import numpy as np
import ml_dtypes


def mxq(x, axis, fmt="e4m3"):
    dtype, down = {"e4m3": (ml_dtypes.float8_e4m3fn, 7), "e5m2": (ml_dtypes.float8_e5m2, 14)}[fmt]
    v = np.moveaxis(np.asarray(x, np.float32).astype(ml_dtypes.bfloat16).astype(np.float64), axis, -1)
    blocks = v.reshape(v.shape[:-1] + (-1, 32))
    amax = np.abs(blocks).max(-1, keepdims=True)
    byte = np.maximum(np.where(amax > 0, np.frexp(amax)[1] - 1 + 127, 0) - down, 1)
    scale = np.exp2(byte - 127.0)
    codes = (blocks / scale).astype(np.float32).astype(dtype).astype(np.float64)
    return np.moveaxis((codes * scale).reshape(v.shape), -1, axis)


WIDE = False


def mx_kscale(k):
    if not WIDE:
        return np.ones(k)
    levels = np.array([10, -10, 5, -5, 0])
    a = np.random.permutation(np.resize(levels, k // 512 * 4)).reshape(k // 512, 4)
    idx = np.arange(k)
    return np.exp2(a[idx // 512, idx % 128 // 32])


BF16 = ml_dtypes.bfloat16


def bf(x):
    return np.asarray(x, np.float32).astype(BF16)


def f64(x):
    return np.asarray(x).astype(np.float64)


E2M1 = np.array([0.0, 0.5, 1.0, 1.5, 2.0, 3.0, 4.0, 6.0, -0.0, -0.5, -1.0, -1.5, -2.0, -3.0, -4.0, -6.0])


def pack_weight(w, fmt):
    k, n = w.shape
    w = f64(bf(w)).reshape(k // 32, 32, n)
    amax = np.abs(w).max(1)
    if fmt == "e4m3":
        byte = np.frexp(amax)[1] - 1 + 127 - 7
    else:
        mant, ex = np.frexp(amax / 6.0)
        byte = np.where(mant > 0.5, ex, ex - 1) + 127
    byte = np.clip(np.where(amax > 0, byte, 1), 1, 254)
    scaled = (w * np.exp2(127.0 - byte)[:, None, :]).reshape(k, n).astype(np.float32)
    by_word = np.ascontiguousarray(scaled.reshape(k // 512, 128, 4, n).transpose(0, 1, 3, 2))
    if fmt == "e4m3":
        words = by_word.astype(ml_dtypes.float8_e4m3fn).view(np.uint8)
    else:
        c = by_word.astype(ml_dtypes.float4_e2m1fn).view(np.uint8) & 0xF
        words = c[..., 0::2] | (c[..., 1::2] << 4)
    return np.ascontiguousarray(words), np.ascontiguousarray(byte.astype(np.uint8).reshape(k // 512, 16, n))


def unpack_weight(words, scales, fmt):
    g, p, n, _ = words.shape
    if fmt == "e4m3":
        vals = np.ascontiguousarray(words).view(ml_dtypes.float8_e4m3fn).astype(np.float64)
    else:
        nib = np.empty((g, p, n, 4), np.uint8)
        nib[..., 0::2] = words & 0xF
        nib[..., 1::2] = words >> 4
        vals = E2M1[nib]
    vals = vals * np.repeat(np.exp2(scales.astype(np.float64) - 127.0), 8, axis=1)[..., None]
    return vals.transpose(0, 1, 3, 2).reshape(g * 512, n)


B, S, D, H, KV, DH, W, KB = 4, 2048, 1024, 1, 1, 128, 128, 512
THETA = 10000.0
FMT = "e4m3"


def rotate_half(t):
    half = t.shape[-1] // 2
    return np.concatenate((-t[..., half:], t[..., :half]), axis=-1)


def rope_cos_sin():
    inv_freq = 1.0 / THETA ** (np.arange(0, DH, 2) / DH)
    ang = np.arange(S)[:, None] * inv_freq[None, :]
    cos = np.repeat(np.cos(ang), 2, axis=-1)[None, :, None, :]
    sin = np.repeat(np.sin(ang), 2, axis=-1)[None, :, None, :]
    return cos, sin


def setup_inputs():
    s = mx_kscale(D)
    x = bf(np.random.standard_normal((B, S, D)) * s)
    Wq_words, Wq_scales = pack_weight(np.random.standard_normal((D, H * DH)) / np.sqrt(D) / s[:, None], FMT)
    Wk_words, Wk_scales = pack_weight(np.random.standard_normal((D, KV * DH)) / np.sqrt(D) / s[:, None], FMT)
    Wv_words, Wv_scales = pack_weight(np.random.standard_normal((D, KV * DH)) * 1.5 / np.sqrt(D) / s[:, None], FMT)
    return {"x": x,
            "Wq_words": Wq_words, "Wq_scales": Wq_scales,
            "Wk_words": Wk_words, "Wk_scales": Wk_scales,
            "Wv_words": Wv_words, "Wv_scales": Wv_scales}


def reference(x, Wq_words, Wq_scales, Wk_words, Wk_scales, Wv_words, Wv_scales):
    cos, sin = rope_cos_sin()
    xq = mxq(f64(x), 2, "e4m3")
    q = (xq @ unpack_weight(Wq_words, Wq_scales, FMT)).reshape(B, S, H, DH)
    k = (xq @ unpack_weight(Wk_words, Wk_scales, FMT)).reshape(B, S, KV, DH)
    v = (xq @ unpack_weight(Wv_words, Wv_scales, FMT)).reshape(B, S, KV, DH)
    q = q * cos + rotate_half(q) * sin
    k = k * cos + rotate_half(k) * sin
    return q.transpose(0, 2, 1, 3), k.transpose(0, 2, 1, 3), v.transpose(0, 2, 1, 3)

@@ -1,0 +1,247 @@
+import math
+from contextlib import ExitStack
+
+import concourse.mybir as mybir
+from concourse.masks import make_identity
+
+BF16 = mybir.dt.bfloat16
+F32 = mybir.dt.float32
+I32 = mybir.dt.int32
+U32 = mybir.dt.uint32
+U8 = mybir.dt.uint8
+FP8X4 = mybir.dt.float8_e4m3fn_x4
+ALU = mybir.AluOpType
+ACT = mybir.ActivationFunctionType
+
+B, S, D, DH = 4, 2048, 1024, 128
+P = 128
+PACK = 4
+K_PASS = P * PACK
+PASSES = D // K_PASS
+ROWS_PER_PARTITION = S // P
+TILES = 4
+ROUNDS_PER_BATCH = ROWS_PER_PARTITION // TILES
+ROUNDS = B * ROUNDS_PER_BATCH
+X_BUFS = 8
+HALF = DH // 2
+FREQS = DH // 2
+THETA = 10000.0
+ROUND_MAGIC = 12582912.0
+
+FLOPS = 2 * B * S * D * 3 * DH
+
+
+def tile_spikinggroupedslidingattention_pa_t_kernel(
+    tc, x, Wq_words, Wq_scales, Wk_words, Wk_scales, Wv_words, Wv_scales, out_0, out_1, out_2
+):
+    nc = tc.nc
+    weights = ((Wq_words, Wq_scales), (Wk_words, Wk_scales), (Wv_words, Wv_scales))
+
+    x_rows = [x[b].rearrange("(j a) k -> j a k", a=ROWS_PER_PARTITION) for b in range(B)]
+    out_rows = [
+        [o[b, 0].rearrange("(j a) i -> j a i", a=ROWS_PER_PARTITION) for b in range(B)]
+        for o in (out_0, out_1, out_2)
+    ]
+
+    with ExitStack() as stack:
+        const = stack.enter_context(tc.tile_pool(name="const", bufs=1))
+        scratch = stack.enter_context(tc.tile_pool(name="scratch", bufs=2))
+        x_pool = stack.enter_context(tc.tile_pool(name="x_pool", bufs=X_BUFS))
+        quant = stack.enter_context(tc.tile_pool(name="quant", bufs=2))
+        rope = stack.enter_context(tc.tile_pool(name="rope", bufs=2))
+        results = stack.enter_context(tc.tile_pool(name="results", bufs=3))
+        xt_banks = stack.enter_context(tc.psum_pool(name="xt_banks", bufs=TILES))
+        qk_banks = stack.enter_context(tc.psum_pool(name="qk_banks", bufs=3))
+        v_banks = stack.enter_context(tc.psum_pool(name="v_banks", bufs=1))
+        stack.enter_context(tc.manual_schedule())
+
+        x_tiles = {}
+        x_codes = {}
+        x_scales = {}
+
+        def load_x(n):
+            b, r = divmod(n, ROUNDS_PER_BATCH)
+            x_sb = x_pool.tile([P, TILES, D], BF16, name="x_sb")
+            nc.sync.dma_start(out=x_sb[:], in_=x_rows[b][:, TILES * r : TILES * (r + 1), :])
+            x_tiles[n] = x_sb
+
+        w_scales = const.tile([P, PASSES, 3 * DH], U8, align_bytes=64)
+        nc.vector.memset(w_scales[:].rearrange("p g n -> p (g n)").bitcast(I32), 0)
+        w_words = const.tile([P, PASSES, 3 * DH], U32, align_bytes=64)
+
+        load_x(0)
+        for w, (words, scales) in enumerate(weights):
+            nc.sync.dma_start(
+                out=w_words[:, :, DH * w : DH * (w + 1)].bitcast(I32),
+                in_=words.rearrange("g p n t -> p g (n t)").bitcast(I32),
+            )
+        load_x(1)
+        for w, (words, scales) in enumerate(weights):
+            for quadrant in range(4):
+                nc.sync.dma_start(
+                    out=w_scales[32 * quadrant : 32 * quadrant + 4, :, DH * w : DH * (w + 1)].bitcast(I32),
+                    in_=scales[:, 4 * quadrant : 4 * quadrant + 4, :].rearrange("g r n -> r g n").bitcast(I32),
+                )
+        for n in range(2, X_BUFS):
+            load_x(n)
+
+        position_int = const.tile([P, ROWS_PER_PARTITION], I32)
+        nc.gpsimd.iota(position_int[:], pattern=[[1, ROWS_PER_PARTITION]], base=0, channel_multiplier=ROWS_PER_PARTITION)
+        identity = const.tile([P, P], F32)
+        make_identity(nc, identity[:])
+
+        turns_per_step = const.tile([P, FREQS], F32)
+        nc.vector.memset(turns_per_step[:], 1.0)
+        nc.vector.tensor_scalar_mul(out=turns_per_step[:], in0=turns_per_step[:], scalar1=1.0 / (2.0 * math.pi))
+        for bit in range(6):
+            with_bit = turns_per_step[:].rearrange("p (h b l) -> p h b l", b=2, l=2**bit)[:, :, 1, :]
+            nc.vector.tensor_scalar_mul(out=with_bit, in0=with_bit, scalar1=THETA ** (-(2.0**bit) / FREQS))
+        quarter_turn = const.tile([P, 1], F32)
+        nc.vector.memset(quarter_turn[:], 1.0)
+        nc.vector.tensor_scalar_mul(out=quarter_turn[:], in0=quarter_turn[:], scalar1=math.pi / 2.0)
+        position = const.tile([P, ROWS_PER_PARTITION], F32)
+        nc.vector.tensor_copy(out=position[:], in_=position_int[:])
+
+        cos_table = const.tile([P, ROWS_PER_PARTITION, DH], F32)
+        sin_table = const.tile([P, ROWS_PER_PARTITION, DH], F32)
+
+        def build_tables(r):
+            tiles = slice(TILES * r, TILES * (r + 1))
+            shape = [P, TILES, FREQS]
+            turns = scratch.tile(shape, F32, name="turns")
+            nc.vector.tensor_tensor(
+                out=turns[:],
+                in0=position[:, tiles].unsqueeze(2).to_broadcast(shape),
+                in1=turns_per_step[:].unsqueeze(1).to_broadcast(shape),
+                op=ALU.mult,
+            )
+            whole = scratch.tile(shape, F32, name="whole")
+            nc.vector.tensor_scalar(
+                out=whole[:], in0=turns[:], scalar1=ROUND_MAGIC, scalar2=ROUND_MAGIC, op0=ALU.add, op1=ALU.subtract
+            )
+            part = scratch.tile(shape, F32, name="part")
+            nc.vector.tensor_tensor(out=part[:], in0=turns[:], in1=whole[:], op=ALU.subtract)
+            minus_abs = scratch.tile(shape, F32, name="minus_abs")
+            nc.vector.scalar_tensor_tensor(
+                out=minus_abs[:], in0=part[:], scalar=-1.0, in1=part[:], op0=ALU.mult, op1=ALU.min
+            )
+            nc.scalar.activation(
+                out=cos_table[:, tiles, :].rearrange("p a (m e) -> p a m e", e=2),
+                in_=minus_abs[:].unsqueeze(3).to_broadcast([P, TILES, FREQS, 2]),
+                func=ACT.Sin,
+                scale=2.0 * math.pi,
+                bias=quarter_turn[:, 0:1],
+            )
+            half_shape = [P, TILES, FREQS // 2, 2]
+            nc.scalar.activation(
+                out=sin_table[:, tiles, 0:HALF].rearrange("p a (m e) -> p a m e", e=2),
+                in_=part[:, :, FREQS // 2 : FREQS].unsqueeze(3).to_broadcast(half_shape),
+                func=ACT.Sin,
+                scale=2.0 * math.pi,
+            )
+            nc.scalar.activation(
+                out=sin_table[:, tiles, HALF:DH].rearrange("p a (m e) -> p a m e", e=2),
+                in_=part[:, :, 0 : FREQS // 2].unsqueeze(3).to_broadcast(half_shape),
+                func=ACT.Sin,
+                scale=-2.0 * math.pi,
+            )
+
+        grouped_tiles = {}
+
+        def transpose_round(n):
+            x_sb = x_tiles[n]
+            grouped = quant.tile([P, TILES, D], BF16, name="grouped", align_bytes=64)
+            for a in range(TILES):
+                pairs = x_sb[:, a, :].bitcast(F32)
+                xt = xt_banks.tile([P, 2 * PASSES, P], F32, name="xt")
+                for g in range(PASSES):
+                    for u in range(2):
+                        nc.tensor.transpose(
+                            xt[:, 2 * g + u, :], pairs[:, 256 * g + u : 256 * (g + 1) : 2], identity[:]
+                        )
+                nc.scalar.copy(
+                    out=grouped[:, a, :].bitcast(F32).rearrange("p (g j u) -> p g j u", g=PASSES, u=2),
+                    in_=xt[:].rearrange("p (g u) j -> p g j u", u=2),
+                )
+            grouped_tiles[n] = grouped
+
+        def quantise_round(n):
+            grouped = grouped_tiles[n]
+            codes = quant.tile([P, TILES * PASSES * P], U32, name="codes", align_bytes=64)
+            scales = quant.tile([P, TILES * PASSES * P], U8, name="scales", align_bytes=64)
+            nc.vector.quantize_mx(
+                out=codes[:].bitcast(FP8X4), scales=scales[:], in_=grouped[:].rearrange("p a c -> p (a c)")
+            )
+            x_codes[n] = codes
+            x_scales[n] = scales
+
+        qk_tiles = {}
+        v_tiles = {}
+
+        def project_round(n):
+            codes = x_codes[n]
+            scales = x_scales[n]
+            v_bank = v_banks.tile([P, TILES, DH], F32, name="v_bank")
+            pairs_of_tiles = []
+            for a in range(TILES):
+                if a % 2 == 0:
+                    qk_bank = qk_banks.tile([P, 2, 2 * DH], F32, name="qk_bank")
+                    pairs_of_tiles.append(qk_bank)
+                for out, columns in ((qk_bank[:, a % 2, :], slice(0, 2 * DH)), (v_bank[:, a, :], slice(2 * DH, 3 * DH))):
+                    for g in range(PASSES):
+                        rows = slice((a * PASSES + g) * P, (a * PASSES + g + 1) * P)
+                        nc.tensor.matmul_mx(
+                            out=out,
+                            lhsT=codes[:, rows].bitcast(FP8X4),
+                            lhsT_scale=scales[:, rows],
+                            rhs=w_words[:, g, columns].bitcast(FP8X4),
+                            rhs_scale=w_scales[:, g, columns],
+                            start=(g == 0),
+                            stop=(g == PASSES - 1),
+                        )
+            qk_tiles[n] = pairs_of_tiles
+            v_tiles[n] = v_bank
+
+        def finish_round(n):
+            b, r = divmod(n, ROUNDS_PER_BATCH)
+            rows = slice(TILES * r, TILES * (r + 1))
+            v_out = results.tile([P, TILES, DH], F32, name="v_out")
+            nc.scalar.copy(out=v_out[:], in_=v_tiles[n][:])
+
+            by_cos = rope.tile([P, 2, TILES, DH], F32, name="by_cos")
+            by_sin = rope.tile([P, 2, TILES, DH], F32, name="by_sin")
+            for pair, qk_bank in enumerate(qk_tiles[n]):
+                two = slice(2 * pair, 2 * pair + 2)
+                table_rows = slice(TILES * r + 2 * pair, TILES * r + 2 * pair + 2)
+                for product, table in ((by_cos, cos_table), (by_sin, sin_table)):
+                    nc.vector.tensor_tensor(
+                        out=product[:, :, two, :].rearrange("p s a i -> p a s i"),
+                        in0=qk_bank[:].rearrange("p a (s i) -> p a s i", s=2),
+                        in1=table[:, table_rows, :].unsqueeze(2).to_broadcast([P, 2, 2, DH]),
+                        op=ALU.mult,
+                    )
+            qk_out = results.tile([P, 2, TILES, DH], F32, name="qk_out")
+            for half in range(2):
+                here = slice(HALF * half, HALF * (half + 1))
+                other = slice(HALF * (1 - half), HALF * (2 - half))
+                nc.gpsimd.tensor_tensor(
+                    out=qk_out[:, :, :, here], in0=by_cos[:, :, :, here], in1=by_sin[:, :, :, other], op=ALU.add
+                )
+            nc.sync.dma_start(out=out_rows[2][b][:, rows, :], in_=v_out[:])
+            nc.sync.dma_start(out=out_rows[0][b][:, rows, :], in_=qk_out[:, 0])
+            nc.sync.dma_start(out=out_rows[1][b][:, rows, :], in_=qk_out[:, 1])
+
+        build_tables(0)
+        transpose_round(0)
+        quantise_round(0)
+        for n in range(ROUNDS):
+            if n + 1 < ROUNDS:
+                transpose_round(n + 1)
+            project_round(n)
+            if n + 1 < ROUNDS:
+                quantise_round(n + 1)
+            if n + X_BUFS < ROUNDS:
+                load_x(n + X_BUFS)
+            finish_round(n)
+            if n + 1 < ROUNDS_PER_BATCH:
+                build_tables(n + 1)

@@ -20,8 +20,12 @@ K_PASS = P * PACK
 PASSES = D // K_PASS
 ROWS_PER_PARTITION = S // P
 TILES = 4
-ROUNDS_PER_BATCH = ROWS_PER_PARTITION // TILES
-ROUNDS = B * ROUNDS_PER_BATCH
+BLOCKS_PER_BATCH = ROWS_PER_PARTITION // TILES
+BLOCKS = B * BLOCKS_PER_BATCH
+RUN = 2
+RUNS_PER_BLOCK = TILES // RUN
+RUNS = BLOCKS * RUNS_PER_BLOCK
+AHEAD = 2
 X_BUFS = 8
 HALF = DH // 2
 FREQS = DH // 2
@@ -47,20 +51,19 @@ def tile_spikinggroupedslidingattention_pa_t_kernel(
         const = stack.enter_context(tc.tile_pool(name="const", bufs=1))
         scratch = stack.enter_context(tc.tile_pool(name="scratch", bufs=2))
         x_pool = stack.enter_context(tc.tile_pool(name="x_pool", bufs=X_BUFS))
-        quant = stack.enter_context(tc.tile_pool(name="quant", bufs=2))
+        grouped_pool = stack.enter_context(tc.tile_pool(name="grouped_pool", bufs=AHEAD + 1))
+        quant = stack.enter_context(tc.tile_pool(name="quant", bufs=AHEAD + 2))
         rope = stack.enter_context(tc.tile_pool(name="rope", bufs=2))
         results = stack.enter_context(tc.tile_pool(name="results", bufs=3))
-        xt_banks = stack.enter_context(tc.psum_pool(name="xt_banks", bufs=TILES))
+        xt_banks = stack.enter_context(tc.psum_pool(name="xt_banks", bufs=AHEAD * RUN))
         qk_banks = stack.enter_context(tc.psum_pool(name="qk_banks", bufs=3))
         v_banks = stack.enter_context(tc.psum_pool(name="v_banks", bufs=1))
         stack.enter_context(tc.manual_schedule())
 
         x_tiles = {}
-        x_codes = {}
-        x_scales = {}
 
         def load_x(n):
-            b, r = divmod(n, ROUNDS_PER_BATCH)
+            b, r = divmod(n, BLOCKS_PER_BATCH)
             x_sb = x_pool.tile([P, TILES, D], BF16, name="x_sb")
             nc.sync.dma_start(out=x_sb[:], in_=x_rows[b][:, TILES * r : TILES * (r + 1), :])
             x_tiles[n] = x_sb
@@ -147,101 +150,112 @@ def tile_spikinggroupedslidingattention_pa_t_kernel(
             )
 
         grouped_tiles = {}
-
-        def transpose_round(n):
-            x_sb = x_tiles[n]
-            grouped = quant.tile([P, TILES, D], BF16, name="grouped", align_bytes=64)
-            for a in range(TILES):
-                pairs = x_sb[:, a, :].bitcast(F32)
-                xt = xt_banks.tile([P, 2 * PASSES, P], F32, name="xt")
-                for g in range(PASSES):
-                    for u in range(2):
-                        nc.tensor.transpose(
-                            xt[:, 2 * g + u, :], pairs[:, 256 * g + u : 256 * (g + 1) : 2], identity[:]
-                        )
-                nc.scalar.copy(
-                    out=grouped[:, a, :].bitcast(F32).rearrange("p (g j u) -> p g j u", g=PASSES, u=2),
-                    in_=xt[:].rearrange("p (g u) j -> p g j u", u=2),
-                )
-            grouped_tiles[n] = grouped
-
-        def quantise_round(n):
-            grouped = grouped_tiles[n]
-            codes = quant.tile([P, TILES * PASSES * P], U32, name="codes", align_bytes=64)
-            scales = quant.tile([P, TILES * PASSES * P], U8, name="scales", align_bytes=64)
-            nc.vector.quantize_mx(
-                out=codes[:].bitcast(FP8X4), scales=scales[:], in_=grouped[:].rearrange("p a c -> p (a c)")
-            )
-            x_codes[n] = codes
-            x_scales[n] = scales
-
+        x_codes = {}
+        x_scales = {}
         qk_tiles = {}
         v_tiles = {}
+        by_cos_tiles = {}
+        by_sin_tiles = {}
 
-        def project_round(n):
-            codes = x_codes[n]
-            scales = x_scales[n]
-            v_bank = v_banks.tile([P, TILES, DH], F32, name="v_bank")
-            pairs_of_tiles = []
-            for a in range(TILES):
-                if a % 2 == 0:
-                    qk_bank = qk_banks.tile([P, 2, 2 * DH], F32, name="qk_bank")
-                    pairs_of_tiles.append(qk_bank)
-                for out, columns in ((qk_bank[:, a % 2, :], slice(0, 2 * DH)), (v_bank[:, a, :], slice(2 * DH, 3 * DH))):
-                    for g in range(PASSES):
-                        rows = slice((a * PASSES + g) * P, (a * PASSES + g + 1) * P)
-                        nc.tensor.matmul_mx(
-                            out=out,
-                            lhsT=codes[:, rows].bitcast(FP8X4),
-                            lhsT_scale=scales[:, rows],
-                            rhs=w_words[:, g, columns].bitcast(FP8X4),
-                            rhs_scale=w_scales[:, g, columns],
-                            start=(g == 0),
-                            stop=(g == PASSES - 1),
+        def transpose_run(u):
+            n, first = divmod(u * RUN, TILES)
+            grouped = grouped_pool.tile([P, RUN, D], BF16, name="grouped", align_bytes=64)
+            for a in range(RUN):
+                pairs = x_tiles[n][:, first + a, :].bitcast(F32)
+                xt = xt_banks.tile([P, 2 * PASSES, P], F32, name="xt")
+                for g in range(PASSES):
+                    for odd in range(2):
+                        nc.tensor.transpose(
+                            xt[:, 2 * g + odd, :], pairs[:, 256 * g + odd : 256 * (g + 1) : 2], identity[:]
                         )
-            qk_tiles[n] = pairs_of_tiles
-            v_tiles[n] = v_bank
+                nc.scalar.copy(
+                    out=grouped[:, a, :].bitcast(F32).rearrange("p (g j o) -> p g j o", g=PASSES, o=2),
+                    in_=xt[:].rearrange("p (g o) j -> p g j o", o=2),
+                )
+            grouped_tiles[u] = grouped
 
-        def finish_round(n):
-            b, r = divmod(n, ROUNDS_PER_BATCH)
+        def quantise_run(u):
+            codes = quant.tile([P, RUN * PASSES * P], U32, name="codes", align_bytes=64)
+            scales = quant.tile([P, RUN * PASSES * P], U8, name="scales", align_bytes=64)
+            nc.vector.quantize_mx(
+                out=codes[:].bitcast(FP8X4), scales=scales[:], in_=grouped_tiles[u][:].rearrange("p a c -> p (a c)")
+            )
+            x_codes[u] = codes
+            x_scales[u] = scales
+
+        def project(u, a, out, columns):
+            for g in range(PASSES):
+                rows = slice((a * PASSES + g) * P, (a * PASSES + g + 1) * P)
+                nc.tensor.matmul_mx(
+                    out=out,
+                    lhsT=x_codes[u][:, rows].bitcast(FP8X4),
+                    lhsT_scale=x_scales[u][:, rows],
+                    rhs=w_words[:, g, columns].bitcast(FP8X4),
+                    rhs_scale=w_scales[:, g, columns],
+                    start=(g == 0),
+                    stop=(g == PASSES - 1),
+                )
+
+        def project_run(u):
+            n, first = divmod(u * RUN, TILES)
+            if first == 0:
+                v_tiles[n] = v_banks.tile([P, TILES, DH], F32, name="v_bank")
+            qk_bank = qk_banks.tile([P, RUN, 2 * DH], F32, name="qk_bank")
+            for a in range(RUN):
+                project(u, a, qk_bank[:, a, :], slice(0, 2 * DH))
+            for a in range(RUN):
+                project(u, a, v_tiles[n][:, first + a, :], slice(2 * DH, 3 * DH))
+            qk_tiles[u] = qk_bank
+
+        def multiply_run(u):
+            n, first = divmod(u * RUN, TILES)
+            if first == 0:
+                by_cos_tiles[n] = rope.tile([P, 2, TILES, DH], F32, name="by_cos")
+                by_sin_tiles[n] = rope.tile([P, 2, TILES, DH], F32, name="by_sin")
+            table_first = TILES * (n % BLOCKS_PER_BATCH) + first
+            for product, table in ((by_cos_tiles[n], cos_table), (by_sin_tiles[n], sin_table)):
+                nc.vector.tensor_tensor(
+                    out=product[:, :, first : first + RUN, :].rearrange("p s a i -> p a s i"),
+                    in0=qk_tiles[u][:].rearrange("p a (s i) -> p a s i", s=2),
+                    in1=table[:, table_first : table_first + RUN, :].unsqueeze(2).to_broadcast([P, RUN, 2, DH]),
+                    op=ALU.mult,
+                )
+
+        def finish_block(n):
+            b, r = divmod(n, BLOCKS_PER_BATCH)
             rows = slice(TILES * r, TILES * (r + 1))
             v_out = results.tile([P, TILES, DH], F32, name="v_out")
             nc.scalar.copy(out=v_out[:], in_=v_tiles[n][:])
-
-            by_cos = rope.tile([P, 2, TILES, DH], F32, name="by_cos")
-            by_sin = rope.tile([P, 2, TILES, DH], F32, name="by_sin")
-            for pair, qk_bank in enumerate(qk_tiles[n]):
-                two = slice(2 * pair, 2 * pair + 2)
-                table_rows = slice(TILES * r + 2 * pair, TILES * r + 2 * pair + 2)
-                for product, table in ((by_cos, cos_table), (by_sin, sin_table)):
-                    nc.vector.tensor_tensor(
-                        out=product[:, :, two, :].rearrange("p s a i -> p a s i"),
-                        in0=qk_bank[:].rearrange("p a (s i) -> p a s i", s=2),
-                        in1=table[:, table_rows, :].unsqueeze(2).to_broadcast([P, 2, 2, DH]),
-                        op=ALU.mult,
-                    )
             qk_out = results.tile([P, 2, TILES, DH], F32, name="qk_out")
             for half in range(2):
                 here = slice(HALF * half, HALF * (half + 1))
                 other = slice(HALF * (1 - half), HALF * (2 - half))
                 nc.gpsimd.tensor_tensor(
-                    out=qk_out[:, :, :, here], in0=by_cos[:, :, :, here], in1=by_sin[:, :, :, other], op=ALU.add
+                    out=qk_out[:, :, :, here],
+                    in0=by_cos_tiles[n][:, :, :, here],
+                    in1=by_sin_tiles[n][:, :, :, other],
+                    op=ALU.add,
                 )
             nc.sync.dma_start(out=out_rows[2][b][:, rows, :], in_=v_out[:])
             nc.sync.dma_start(out=out_rows[0][b][:, rows, :], in_=qk_out[:, 0])
             nc.sync.dma_start(out=out_rows[1][b][:, rows, :], in_=qk_out[:, 1])
 
         build_tables(0)
-        transpose_round(0)
-        quantise_round(0)
-        for n in range(ROUNDS):
-            if n + 1 < ROUNDS:
-                transpose_round(n + 1)
-            project_round(n)
-            if n + 1 < ROUNDS:
-                quantise_round(n + 1)
-            if n + X_BUFS < ROUNDS:
-                load_x(n + X_BUFS)
-            finish_round(n)
-            if n + 1 < ROUNDS_PER_BATCH:
-                build_tables(n + 1)
+        for u in range(AHEAD):
+            transpose_run(u)
+        for u in range(AHEAD):
+            quantise_run(u)
+        for u in range(RUNS):
+            if u + AHEAD < RUNS:
+                transpose_run(u + AHEAD)
+            project_run(u)
+            if u + AHEAD < RUNS:
+                quantise_run(u + AHEAD)
+            multiply_run(u)
+            n, run_in_block = divmod(u, RUNS_PER_BLOCK)
+            if run_in_block == RUNS_PER_BLOCK - 1:
+                if n + X_BUFS < BLOCKS:
+                    load_x(n + X_BUFS)
+                finish_block(n)
+                if n + 1 < BLOCKS_PER_BATCH:
+                    build_tables(n + 1)

@@ -27,6 +27,7 @@ RUNS_PER_BLOCK = TILES // RUN
 RUNS = BLOCKS * RUNS_PER_BLOCK
 AHEAD = 2
 X_BUFS = 8
+HEAD_BLOCKS = 2
 HALF = DH // 2
 FREQS = DH // 2
 THETA = 10000.0
@@ -49,7 +50,6 @@ def tile_spikinggroupedslidingattention_pa_t_kernel(
 
     with ExitStack() as stack:
         const = stack.enter_context(tc.tile_pool(name="const", bufs=1))
-        scratch = stack.enter_context(tc.tile_pool(name="scratch", bufs=2))
         x_pool = stack.enter_context(tc.tile_pool(name="x_pool", bufs=X_BUFS))
         grouped_pool = stack.enter_context(tc.tile_pool(name="grouped_pool", bufs=AHEAD + 1))
         quant = stack.enter_context(tc.tile_pool(name="quant", bufs=AHEAD + 2))
@@ -62,36 +62,42 @@ def tile_spikinggroupedslidingattention_pa_t_kernel(
 
         x_tiles = {}
 
-        def load_x(n):
+        def load_x(n, first, count):
             b, r = divmod(n, BLOCKS_PER_BATCH)
-            x_sb = x_pool.tile([P, TILES, D], BF16, name="x_sb")
-            nc.sync.dma_start(out=x_sb[:], in_=x_rows[b][:, TILES * r : TILES * (r + 1), :])
-            x_tiles[n] = x_sb
+            if first == 0:
+                x_tiles[n] = x_pool.tile([P, TILES, D], BF16, name="x_sb")
+            nc.sync.dma_start(
+                out=x_tiles[n][:, first : first + count, :],
+                in_=x_rows[b][:, TILES * r + first : TILES * r + first + count, :],
+            )
+
+        position_int = const.tile([P, ROWS_PER_PARTITION], I32)
+        nc.gpsimd.iota(position_int[:], pattern=[[1, ROWS_PER_PARTITION]], base=0, channel_multiplier=ROWS_PER_PARTITION)
+        identity = const.tile([P, P], F32)
+        make_identity(nc, identity[:])
+
+        w_words = const.tile([P, PASSES, 3 * DH], U32, align_bytes=64)
+        for w, (words, scales) in enumerate(weights):
+            nc.gpsimd.dma_start(
+                out=w_words[:, :, DH * w : DH * (w + 1)].bitcast(F32),
+                in_=words.rearrange("g p n t -> p g (n t)").bitcast(F32),
+            )
 
         w_scales = const.tile([P, PASSES, 3 * DH], U8, align_bytes=64)
         nc.vector.memset(w_scales[:].rearrange("p g n -> p (g n)").bitcast(I32), 0)
-        w_words = const.tile([P, PASSES, 3 * DH], U32, align_bytes=64)
 
-        load_x(0)
-        for w, (words, scales) in enumerate(weights):
-            nc.sync.dma_start(
-                out=w_words[:, :, DH * w : DH * (w + 1)].bitcast(I32),
-                in_=words.rearrange("g p n t -> p g (n t)").bitcast(I32),
-            )
-        load_x(1)
+        load_x(0, 0, RUN)
+        load_x(0, RUN, RUN)
+        load_x(1, 0, RUN)
         for w, (words, scales) in enumerate(weights):
             for quadrant in range(4):
                 nc.sync.dma_start(
                     out=w_scales[32 * quadrant : 32 * quadrant + 4, :, DH * w : DH * (w + 1)].bitcast(I32),
                     in_=scales[:, 4 * quadrant : 4 * quadrant + 4, :].rearrange("g r n -> r g n").bitcast(I32),
                 )
-        for n in range(2, X_BUFS):
-            load_x(n)
-
-        position_int = const.tile([P, ROWS_PER_PARTITION], I32)
-        nc.gpsimd.iota(position_int[:], pattern=[[1, ROWS_PER_PARTITION]], base=0, channel_multiplier=ROWS_PER_PARTITION)
-        identity = const.tile([P, P], F32)
-        make_identity(nc, identity[:])
+        load_x(1, RUN, RUN)
+        for n in range(HEAD_BLOCKS, X_BUFS):
+            load_x(n, 0, TILES)
 
         turns_per_step = const.tile([P, FREQS], F32)
         nc.vector.memset(turns_per_step[:], 1.0)
@@ -108,29 +114,43 @@ def tile_spikinggroupedslidingattention_pa_t_kernel(
         cos_table = const.tile([P, ROWS_PER_PARTITION, DH], F32)
         sin_table = const.tile([P, ROWS_PER_PARTITION, DH], F32)
 
-        def build_tables(r):
-            tiles = slice(TILES * r, TILES * (r + 1))
-            shape = [P, TILES, FREQS]
-            turns = scratch.tile(shape, F32, name="turns")
+        turns = const.tile([P, ROWS_PER_PARTITION, FREQS], F32)
+        whole = const.tile([P, ROWS_PER_PARTITION, FREQS], F32)
+        part = const.tile([P, ROWS_PER_PARTITION, FREQS], F32)
+        minus_abs = const.tile([P, ROWS_PER_PARTITION, FREQS], F32)
+
+        def build_angles(first, count):
+            tiles = slice(first, first + count)
+            shape = [P, count, FREQS]
             nc.vector.tensor_tensor(
-                out=turns[:],
+                out=turns[:, tiles, :],
                 in0=position[:, tiles].unsqueeze(2).to_broadcast(shape),
                 in1=turns_per_step[:].unsqueeze(1).to_broadcast(shape),
                 op=ALU.mult,
             )
-            whole = scratch.tile(shape, F32, name="whole")
             nc.vector.tensor_scalar(
-                out=whole[:], in0=turns[:], scalar1=ROUND_MAGIC, scalar2=ROUND_MAGIC, op0=ALU.add, op1=ALU.subtract
+                out=whole[:, tiles, :],
+                in0=turns[:, tiles, :],
+                scalar1=ROUND_MAGIC,
+                scalar2=ROUND_MAGIC,
+                op0=ALU.add,
+                op1=ALU.subtract,
             )
-            part = scratch.tile(shape, F32, name="part")
-            nc.vector.tensor_tensor(out=part[:], in0=turns[:], in1=whole[:], op=ALU.subtract)
-            minus_abs = scratch.tile(shape, F32, name="minus_abs")
+            nc.vector.tensor_tensor(out=part[:, tiles, :], in0=turns[:, tiles, :], in1=whole[:, tiles, :], op=ALU.subtract)
             nc.vector.scalar_tensor_tensor(
-                out=minus_abs[:], in0=part[:], scalar=-1.0, in1=part[:], op0=ALU.mult, op1=ALU.min
+                out=minus_abs[:, tiles, :],
+                in0=part[:, tiles, :],
+                scalar=-1.0,
+                in1=part[:, tiles, :],
+                op0=ALU.mult,
+                op1=ALU.min,
             )
+
+        def build_tables(r):
+            tiles = slice(TILES * r, TILES * (r + 1))
             nc.scalar.activation(
                 out=cos_table[:, tiles, :].rearrange("p a (m e) -> p a m e", e=2),
-                in_=minus_abs[:].unsqueeze(3).to_broadcast([P, TILES, FREQS, 2]),
+                in_=minus_abs[:, tiles, :].unsqueeze(3).to_broadcast([P, TILES, FREQS, 2]),
                 func=ACT.Sin,
                 scale=2.0 * math.pi,
                 bias=quarter_turn[:, 0:1],
@@ -138,13 +158,13 @@ def tile_spikinggroupedslidingattention_pa_t_kernel(
             half_shape = [P, TILES, FREQS // 2, 2]
             nc.scalar.activation(
                 out=sin_table[:, tiles, 0:HALF].rearrange("p a (m e) -> p a m e", e=2),
-                in_=part[:, :, FREQS // 2 : FREQS].unsqueeze(3).to_broadcast(half_shape),
+                in_=part[:, tiles, FREQS // 2 : FREQS].unsqueeze(3).to_broadcast(half_shape),
                 func=ACT.Sin,
                 scale=2.0 * math.pi,
             )
             nc.scalar.activation(
                 out=sin_table[:, tiles, HALF:DH].rearrange("p a (m e) -> p a m e", e=2),
-                in_=part[:, :, 0 : FREQS // 2].unsqueeze(3).to_broadcast(half_shape),
+                in_=part[:, tiles, 0 : FREQS // 2].unsqueeze(3).to_broadcast(half_shape),
                 func=ACT.Sin,
                 scale=-2.0 * math.pi,
             )
@@ -221,26 +241,34 @@ def tile_spikinggroupedslidingattention_pa_t_kernel(
                     op=ALU.mult,
                 )
 
-        def finish_block(n):
+        qk_out_tiles = {}
+
+        def add_products(engine, n, first, count):
+            if first == 0:
+                qk_out_tiles[n] = results.tile([P, 2, TILES, DH], F32, name="qk_out")
+            tiles = slice(first, first + count)
+            for half in range(2):
+                here = slice(HALF * half, HALF * (half + 1))
+                other = slice(HALF * (1 - half), HALF * (2 - half))
+                engine.tensor_tensor(
+                    out=qk_out_tiles[n][:, :, tiles, here],
+                    in0=by_cos_tiles[n][:, :, tiles, here],
+                    in1=by_sin_tiles[n][:, :, tiles, other],
+                    op=ALU.add,
+                )
+
+        def store_block(n):
             b, r = divmod(n, BLOCKS_PER_BATCH)
             rows = slice(TILES * r, TILES * (r + 1))
             v_out = results.tile([P, TILES, DH], F32, name="v_out")
             nc.scalar.copy(out=v_out[:], in_=v_tiles[n][:])
-            qk_out = results.tile([P, 2, TILES, DH], F32, name="qk_out")
-            for half in range(2):
-                here = slice(HALF * half, HALF * (half + 1))
-                other = slice(HALF * (1 - half), HALF * (2 - half))
-                nc.gpsimd.tensor_tensor(
-                    out=qk_out[:, :, :, here],
-                    in0=by_cos_tiles[n][:, :, :, here],
-                    in1=by_sin_tiles[n][:, :, :, other],
-                    op=ALU.add,
-                )
             nc.sync.dma_start(out=out_rows[2][b][:, rows, :], in_=v_out[:])
-            nc.sync.dma_start(out=out_rows[0][b][:, rows, :], in_=qk_out[:, 0])
-            nc.sync.dma_start(out=out_rows[1][b][:, rows, :], in_=qk_out[:, 1])
+            nc.sync.dma_start(out=out_rows[0][b][:, rows, :], in_=qk_out_tiles[n][:, 0])
+            nc.sync.dma_start(out=out_rows[1][b][:, rows, :], in_=qk_out_tiles[n][:, 1])
 
+        build_angles(0, TILES)
         build_tables(0)
+        build_angles(TILES, ROWS_PER_PARTITION - TILES)
         for u in range(AHEAD):
             transpose_run(u)
         for u in range(AHEAD):
@@ -253,9 +281,14 @@ def tile_spikinggroupedslidingattention_pa_t_kernel(
                 quantise_run(u + AHEAD)
             multiply_run(u)
             n, run_in_block = divmod(u, RUNS_PER_BLOCK)
-            if run_in_block == RUNS_PER_BLOCK - 1:
+            last_run_of_block = run_in_block == RUNS_PER_BLOCK - 1
+            if n == BLOCKS - 1:
+                add_products(nc.vector, n, RUN * run_in_block, RUN)
+            elif last_run_of_block:
+                add_products(nc.gpsimd, n, 0, TILES)
+            if last_run_of_block:
                 if n + X_BUFS < BLOCKS:
-                    load_x(n + X_BUFS)
-                finish_block(n)
+                    load_x(n + X_BUFS, 0, TILES)
+                store_block(n)
                 if n + 1 < BLOCKS_PER_BATCH:
                     build_tables(n + 1)

@@ -26,6 +26,7 @@ RUN = 2
 RUNS_PER_BLOCK = TILES // RUN
 RUNS = BLOCKS * RUNS_PER_BLOCK
 AHEAD = 2
+BUNCH = 2
 X_BUFS = 8
 HEAD_BLOCKS = 2
 HALF = DH // 2
@@ -86,16 +87,17 @@ def tile_spikinggroupedslidingattention_pa_t_kernel(
         w_scales = const.tile([P, PASSES, 3 * DH], U8, align_bytes=64)
         nc.vector.memset(w_scales[:].rearrange("p g n -> p (g n)").bitcast(I32), 0)
 
-        load_x(0, 0, RUN)
-        load_x(0, RUN, RUN)
-        load_x(1, 0, RUN)
+        head_runs = [divmod(u, RUNS_PER_BLOCK) for u in range(HEAD_BLOCKS * RUNS_PER_BLOCK)]
+        for n, run_in_block in head_runs[: AHEAD + BUNCH]:
+            load_x(n, RUN * run_in_block, RUN)
         for w, (words, scales) in enumerate(weights):
             for quadrant in range(4):
                 nc.sync.dma_start(
                     out=w_scales[32 * quadrant : 32 * quadrant + 4, :, DH * w : DH * (w + 1)].bitcast(I32),
                     in_=scales[:, 4 * quadrant : 4 * quadrant + 4, :].rearrange("g r n -> r g n").bitcast(I32),
                 )
-        load_x(1, RUN, RUN)
+        for n, run_in_block in head_runs[AHEAD + BUNCH :]:
+            load_x(n, RUN * run_in_block, RUN)
         for n in range(HEAD_BLOCKS, X_BUFS):
             load_x(n, 0, TILES)
 
@@ -273,22 +275,26 @@ def tile_spikinggroupedslidingattention_pa_t_kernel(
             transpose_run(u)
         for u in range(AHEAD):
             quantise_run(u)
-        for u in range(RUNS):
-            if u + AHEAD < RUNS:
-                transpose_run(u + AHEAD)
-            project_run(u)
-            if u + AHEAD < RUNS:
-                quantise_run(u + AHEAD)
-            multiply_run(u)
-            n, run_in_block = divmod(u, RUNS_PER_BLOCK)
-            last_run_of_block = run_in_block == RUNS_PER_BLOCK - 1
-            if n == BLOCKS - 1:
-                add_products(nc.vector, n, RUN * run_in_block, RUN)
-            elif last_run_of_block:
-                add_products(nc.gpsimd, n, 0, TILES)
-            if last_run_of_block:
-                if n + X_BUFS < BLOCKS:
-                    load_x(n + X_BUFS, 0, TILES)
-                store_block(n)
-                if n + 1 < BLOCKS_PER_BATCH:
-                    build_tables(n + 1)
+        for first_run in range(0, RUNS, BUNCH):
+            bunch = range(first_run, first_run + BUNCH)
+            ahead = [u + AHEAD for u in bunch if u + AHEAD < RUNS]
+            for u in ahead:
+                transpose_run(u)
+            for u in bunch:
+                project_run(u)
+            for u in ahead:
+                quantise_run(u)
+            for u in bunch:
+                multiply_run(u)
+                n, run_in_block = divmod(u, RUNS_PER_BLOCK)
+                last_run_of_block = run_in_block == RUNS_PER_BLOCK - 1
+                if n == BLOCKS - 1:
+                    add_products(nc.vector, n, RUN * run_in_block, RUN)
+                elif last_run_of_block:
+                    add_products(nc.gpsimd, n, 0, TILES)
+                if last_run_of_block:
+                    if n + X_BUFS < BLOCKS:
+                        load_x(n + X_BUFS, 0, TILES)
+                    store_block(n)
+                    if n + 1 < BLOCKS_PER_BATCH:
+                        build_tables(n + 1)

@@ -26,9 +26,10 @@ RUN = 2
 RUNS_PER_BLOCK = TILES // RUN
 RUNS = BLOCKS * RUNS_PER_BLOCK
 AHEAD = 2
-BUNCH = 2
 X_BUFS = 8
 HEAD_BLOCKS = 2
+TAIL_BLOCKS = 2
+V_LAG = 4
 HALF = DH // 2
 FREQS = DH // 2
 THETA = 10000.0
@@ -53,7 +54,7 @@ def tile_spikinggroupedslidingattention_pa_t_kernel(
         const = stack.enter_context(tc.tile_pool(name="const", bufs=1))
         x_pool = stack.enter_context(tc.tile_pool(name="x_pool", bufs=X_BUFS))
         grouped_pool = stack.enter_context(tc.tile_pool(name="grouped_pool", bufs=AHEAD + 1))
-        quant = stack.enter_context(tc.tile_pool(name="quant", bufs=AHEAD + 2))
+        quant = stack.enter_context(tc.tile_pool(name="quant", bufs=AHEAD + V_LAG + 2))
         rope = stack.enter_context(tc.tile_pool(name="rope", bufs=2))
         results = stack.enter_context(tc.tile_pool(name="results", bufs=3))
         xt_banks = stack.enter_context(tc.psum_pool(name="xt_banks", bufs=AHEAD * RUN))
@@ -87,17 +88,16 @@ def tile_spikinggroupedslidingattention_pa_t_kernel(
         w_scales = const.tile([P, PASSES, 3 * DH], U8, align_bytes=64)
         nc.vector.memset(w_scales[:].rearrange("p g n -> p (g n)").bitcast(I32), 0)
 
-        head_runs = [divmod(u, RUNS_PER_BLOCK) for u in range(HEAD_BLOCKS * RUNS_PER_BLOCK)]
-        for n, run_in_block in head_runs[: AHEAD + BUNCH]:
-            load_x(n, RUN * run_in_block, RUN)
+        load_x(0, 0, RUN)
+        load_x(0, RUN, RUN)
+        load_x(1, 0, RUN)
         for w, (words, scales) in enumerate(weights):
             for quadrant in range(4):
                 nc.sync.dma_start(
                     out=w_scales[32 * quadrant : 32 * quadrant + 4, :, DH * w : DH * (w + 1)].bitcast(I32),
                     in_=scales[:, 4 * quadrant : 4 * quadrant + 4, :].rearrange("g r n -> r g n").bitcast(I32),
                 )
-        for n, run_in_block in head_runs[AHEAD + BUNCH :]:
-            load_x(n, RUN * run_in_block, RUN)
+        load_x(1, RUN, RUN)
         for n in range(HEAD_BLOCKS, X_BUFS):
             load_x(n, 0, TILES)
 
@@ -218,16 +218,23 @@ def tile_spikinggroupedslidingattention_pa_t_kernel(
                     stop=(g == PASSES - 1),
                 )
 
-        def project_run(u):
-            n, first = divmod(u * RUN, TILES)
-            if first == 0:
-                v_tiles[n] = v_banks.tile([P, TILES, DH], F32, name="v_bank")
+        def project_qk(u):
             qk_bank = qk_banks.tile([P, RUN, 2 * DH], F32, name="qk_bank")
             for a in range(RUN):
                 project(u, a, qk_bank[:, a, :], slice(0, 2 * DH))
+            qk_tiles[u] = qk_bank
+
+        def project_v(u):
+            n, first = divmod(u * RUN, TILES)
+            if first == 0:
+                v_tiles[n] = v_banks.tile([P, TILES, DH], F32, name="v_bank")
             for a in range(RUN):
                 project(u, a, v_tiles[n][:, first + a, :], slice(2 * DH, 3 * DH))
-            qk_tiles[u] = qk_bank
+            if first + RUN == TILES:
+                b, r = divmod(n, BLOCKS_PER_BATCH)
+                v_out = results.tile([P, TILES, DH], F32, name="v_out")
+                nc.scalar.copy(out=v_out[:], in_=v_tiles[n][:])
+                nc.sync.dma_start(out=out_rows[2][b][:, TILES * r : TILES * (r + 1), :], in_=v_out[:])
 
         def multiply_run(u):
             n, first = divmod(u * RUN, TILES)
@@ -243,30 +250,22 @@ def tile_spikinggroupedslidingattention_pa_t_kernel(
                     op=ALU.mult,
                 )
 
-        qk_out_tiles = {}
-
-        def add_products(engine, n, first, count):
-            if first == 0:
-                qk_out_tiles[n] = results.tile([P, 2, TILES, DH], F32, name="qk_out")
+        def finish_qk(engine, n, first, count):
+            b, r = divmod(n, BLOCKS_PER_BATCH)
             tiles = slice(first, first + count)
+            rows = slice(TILES * r + first, TILES * r + first + count)
+            qk_out = results.tile([P, 2, count, DH], F32, name="qk_out")
             for half in range(2):
                 here = slice(HALF * half, HALF * (half + 1))
                 other = slice(HALF * (1 - half), HALF * (2 - half))
                 engine.tensor_tensor(
-                    out=qk_out_tiles[n][:, :, tiles, here],
+                    out=qk_out[:, :, :, here],
                     in0=by_cos_tiles[n][:, :, tiles, here],
                     in1=by_sin_tiles[n][:, :, tiles, other],
                     op=ALU.add,
                 )
-
-        def store_block(n):
-            b, r = divmod(n, BLOCKS_PER_BATCH)
-            rows = slice(TILES * r, TILES * (r + 1))
-            v_out = results.tile([P, TILES, DH], F32, name="v_out")
-            nc.scalar.copy(out=v_out[:], in_=v_tiles[n][:])
-            nc.sync.dma_start(out=out_rows[2][b][:, rows, :], in_=v_out[:])
-            nc.sync.dma_start(out=out_rows[0][b][:, rows, :], in_=qk_out_tiles[n][:, 0])
-            nc.sync.dma_start(out=out_rows[1][b][:, rows, :], in_=qk_out_tiles[n][:, 1])
+            nc.sync.dma_start(out=out_rows[0][b][:, rows, :], in_=qk_out[:, 0])
+            nc.sync.dma_start(out=out_rows[1][b][:, rows, :], in_=qk_out[:, 1])
 
         build_angles(0, TILES)
         build_tables(0)
@@ -275,26 +274,27 @@ def tile_spikinggroupedslidingattention_pa_t_kernel(
             transpose_run(u)
         for u in range(AHEAD):
             quantise_run(u)
-        for first_run in range(0, RUNS, BUNCH):
-            bunch = range(first_run, first_run + BUNCH)
-            ahead = [u + AHEAD for u in bunch if u + AHEAD < RUNS]
-            for u in ahead:
-                transpose_run(u)
-            for u in bunch:
-                project_run(u)
-            for u in ahead:
-                quantise_run(u)
-            for u in bunch:
+        for u in range(RUNS + V_LAG):
+            if u + AHEAD < RUNS:
+                transpose_run(u + AHEAD)
+            if u < RUNS:
+                project_qk(u)
+            if u >= V_LAG:
+                project_v(u - V_LAG)
+            if u + AHEAD < RUNS:
+                quantise_run(u + AHEAD)
+            if u < RUNS:
                 multiply_run(u)
                 n, run_in_block = divmod(u, RUNS_PER_BLOCK)
                 last_run_of_block = run_in_block == RUNS_PER_BLOCK - 1
-                if n == BLOCKS - 1:
-                    add_products(nc.vector, n, RUN * run_in_block, RUN)
+                if u == RUNS - 1:
+                    finish_qk(nc.vector, n, RUN * run_in_block, RUN)
+                elif n >= BLOCKS - TAIL_BLOCKS:
+                    finish_qk(nc.gpsimd, n, RUN * run_in_block, RUN)
                 elif last_run_of_block:
-                    add_products(nc.gpsimd, n, 0, TILES)
+                    finish_qk(nc.gpsimd, n, 0, TILES)
                 if last_run_of_block:
                     if n + X_BUFS < BLOCKS:
                         load_x(n + X_BUFS, 0, TILES)
-                    store_block(n)
                     if n + 1 < BLOCKS_PER_BATCH:
                         build_tables(n + 1)

@@ -29,6 +29,8 @@ AHEAD = 2
 X_BUFS = 8
 HEAD_BLOCKS = 2
 TAIL_BLOCKS = 2
+SORTED = 1
+FIRST_SORTED_RUN = 4
 V_LAG = 4
 HALF = DH // 2
 FREQS = DH // 2
@@ -53,6 +55,7 @@ def tile_spikinggroupedslidingattention_pa_t_kernel(
     with ExitStack() as stack:
         const = stack.enter_context(tc.tile_pool(name="const", bufs=1))
         x_pool = stack.enter_context(tc.tile_pool(name="x_pool", bufs=X_BUFS))
+        sorted_pool = stack.enter_context(tc.tile_pool(name="sorted_pool", bufs=3))
         grouped_pool = stack.enter_context(tc.tile_pool(name="grouped_pool", bufs=AHEAD + 1))
         quant = stack.enter_context(tc.tile_pool(name="quant", bufs=AHEAD + V_LAG + 2))
         rope = stack.enter_context(tc.tile_pool(name="rope", bufs=2))
@@ -88,7 +91,8 @@ def tile_spikinggroupedslidingattention_pa_t_kernel(
         w_scales = const.tile([P, PASSES, 3 * DH], U8, align_bytes=64)
         nc.vector.memset(w_scales[:].rearrange("p g n -> p (g n)").bitcast(I32), 0)
 
-        load_x(0, 0, RUN)
+        load_x(0, 0, 1)
+        load_x(0, 1, 1)
         load_x(0, RUN, RUN)
         load_x(1, 0, RUN)
         for w, (words, scales) in enumerate(weights):
@@ -179,6 +183,18 @@ def tile_spikinggroupedslidingattention_pa_t_kernel(
         by_cos_tiles = {}
         by_sin_tiles = {}
 
+        sorted_tiles = {}
+
+        def sort_run(u):
+            n, first = divmod(u * RUN, TILES)
+            for a in range(SORTED):
+                in_order = sorted_pool.tile([P, D // 2], F32, name="in_order")
+                nc.scalar.copy(
+                    out=in_order[:].rearrange("p (g o j) -> p g o j", g=PASSES, o=2),
+                    in_=x_tiles[n][:, first + a, :].bitcast(F32).rearrange("p (g j o) -> p g o j", g=PASSES, o=2),
+                )
+                sorted_tiles[(u, a)] = in_order
+
         def transpose_run(u):
             n, first = divmod(u * RUN, TILES)
             grouped = grouped_pool.tile([P, RUN, D], BF16, name="grouped", align_bytes=64)
@@ -187,9 +203,11 @@ def tile_spikinggroupedslidingattention_pa_t_kernel(
                 xt = xt_banks.tile([P, 2 * PASSES, P], F32, name="xt")
                 for g in range(PASSES):
                     for odd in range(2):
-                        nc.tensor.transpose(
-                            xt[:, 2 * g + odd, :], pairs[:, 256 * g + odd : 256 * (g + 1) : 2], identity[:]
-                        )
+                        if (u, a) in sorted_tiles:
+                            words = sorted_tiles[(u, a)][:, P * (2 * g + odd) : P * (2 * g + odd + 1)]
+                        else:
+                            words = pairs[:, 256 * g + odd : 256 * (g + 1) : 2]
+                        nc.tensor.transpose(xt[:, 2 * g + odd, :], words, identity[:])
                 nc.scalar.copy(
                     out=grouped[:, a, :].bitcast(F32).rearrange("p (g j o) -> p g j o", g=PASSES, o=2),
                     in_=xt[:].rearrange("p (g o) j -> p g j o", o=2),
@@ -275,6 +293,8 @@ def tile_spikinggroupedslidingattention_pa_t_kernel(
         for u in range(AHEAD):
             quantise_run(u)
         for u in range(RUNS + V_LAG):
+            if FIRST_SORTED_RUN <= u + AHEAD + 1 < RUNS:
+                sort_run(u + AHEAD + 1)
             if u + AHEAD < RUNS:
                 transpose_run(u + AHEAD)
             if u < RUNS:

@@ -60,6 +60,7 @@ def tile_spikinggroupedslidingattention_pa_t_kernel(
         quant = stack.enter_context(tc.tile_pool(name="quant", bufs=AHEAD + V_LAG + 2))
         rope = stack.enter_context(tc.tile_pool(name="rope", bufs=2))
         results = stack.enter_context(tc.tile_pool(name="results", bufs=3))
+        last_v = stack.enter_context(tc.tile_pool(name="last_v", bufs=V_LAG))
         xt_banks = stack.enter_context(tc.psum_pool(name="xt_banks", bufs=AHEAD * RUN))
         qk_banks = stack.enter_context(tc.psum_pool(name="qk_banks", bufs=3))
         v_banks = stack.enter_context(tc.psum_pool(name="v_banks", bufs=1))
@@ -244,12 +245,20 @@ def tile_spikinggroupedslidingattention_pa_t_kernel(
 
         def project_v(u):
             n, first = divmod(u * RUN, TILES)
+            b, r = divmod(n, BLOCKS_PER_BATCH)
+            if u >= RUNS - V_LAG:
+                v_bank = xt_banks.tile([P, RUN, DH], F32, name="xt")
+                for a in range(RUN):
+                    project(u, a, v_bank[:, a, :], slice(2 * DH, 3 * DH))
+                v_last = last_v.tile([P, RUN, DH], F32, name="v_last")
+                nc.scalar.copy(out=v_last[:], in_=v_bank[:])
+                nc.sync.dma_start(out=out_rows[2][b][:, TILES * r + first : TILES * r + first + RUN, :], in_=v_last[:])
+                return
             if first == 0:
                 v_tiles[n] = v_banks.tile([P, TILES, DH], F32, name="v_bank")
             for a in range(RUN):
                 project(u, a, v_tiles[n][:, first + a, :], slice(2 * DH, 3 * DH))
             if first + RUN == TILES:
-                b, r = divmod(n, BLOCKS_PER_BATCH)
                 v_out = results.tile([P, TILES, DH], F32, name="v_out")
                 nc.scalar.copy(out=v_out[:], in_=v_tiles[n][:])
                 nc.sync.dma_start(out=out_rows[2][b][:, TILES * r : TILES * (r + 1), :], in_=v_out[:])
@@ -293,7 +302,7 @@ def tile_spikinggroupedslidingattention_pa_t_kernel(
         for u in range(AHEAD):
             quantise_run(u)
         for u in range(RUNS + V_LAG):
-            if FIRST_SORTED_RUN <= u + AHEAD + 1 < RUNS:
+            if FIRST_SORTED_RUN <= u + AHEAD + 1 < RUNS and (u + AHEAD + 1) % RUNS_PER_BLOCK == 0:
                 sort_run(u + AHEAD + 1)
             if u + AHEAD < RUNS:
                 transpose_run(u + AHEAD)

@@ -266,33 +266,36 @@ def tile_spikinggroupedslidingattention_pa_t_kernel(
         def multiply_run(u):
             n, first = divmod(u * RUN, TILES)
             if first == 0:
-                by_cos_tiles[n] = rope.tile([P, 2, TILES, DH], F32, name="by_cos")
-                by_sin_tiles[n] = rope.tile([P, 2, TILES, DH], F32, name="by_sin")
+                by_cos_tiles[n] = rope.tile([P, TILES, 2, DH], F32, name="by_cos")
+                by_sin_tiles[n] = rope.tile([P, TILES, 2, DH], F32, name="by_sin")
             table_first = TILES * (n % BLOCKS_PER_BATCH) + first
             for product, table in ((by_cos_tiles[n], cos_table), (by_sin_tiles[n], sin_table)):
                 nc.vector.tensor_tensor(
-                    out=product[:, :, first : first + RUN, :].rearrange("p s a i -> p a s i"),
+                    out=product[:, first : first + RUN, :, :],
                     in0=qk_tiles[u][:].rearrange("p a (s i) -> p a s i", s=2),
                     in1=table[:, table_first : table_first + RUN, :].unsqueeze(2).to_broadcast([P, RUN, 2, DH]),
                     op=ALU.mult,
                 )
 
-        def finish_qk(engine, n, first, count):
+        qk_out_tiles = {}
+
+        def add_run(engine, u):
+            n, first = divmod(u * RUN, TILES)
+            if first == 0:
+                qk_out_tiles[n] = results.tile([P, 2, TILES, DH], F32, name="qk_out")
+            tiles = slice(first, first + RUN)
+            engine.tensor_tensor(
+                out=qk_out_tiles[n][:, :, tiles, :].rearrange("p s a (h i) -> p a s h i", h=2),
+                in0=by_cos_tiles[n][:, tiles, :, :].rearrange("p a s (h i) -> p a s h i", h=2),
+                in1=by_sin_tiles[n][:, tiles, :, :].rearrange("p a s (h i) -> p a s h i", h=2)[:, :, :, ::-1, :],
+                op=ALU.add,
+            )
+
+        def store_qk(n, first, count):
             b, r = divmod(n, BLOCKS_PER_BATCH)
-            tiles = slice(first, first + count)
             rows = slice(TILES * r + first, TILES * r + first + count)
-            qk_out = results.tile([P, 2, count, DH], F32, name="qk_out")
-            for half in range(2):
-                here = slice(HALF * half, HALF * (half + 1))
-                other = slice(HALF * (1 - half), HALF * (2 - half))
-                engine.tensor_tensor(
-                    out=qk_out[:, :, :, here],
-                    in0=by_cos_tiles[n][:, :, tiles, here],
-                    in1=by_sin_tiles[n][:, :, tiles, other],
-                    op=ALU.add,
-                )
-            nc.sync.dma_start(out=out_rows[0][b][:, rows, :], in_=qk_out[:, 0])
-            nc.sync.dma_start(out=out_rows[1][b][:, rows, :], in_=qk_out[:, 1])
+            nc.sync.dma_start(out=out_rows[0][b][:, rows, :], in_=qk_out_tiles[n][:, 0, first : first + count, :])
+            nc.sync.dma_start(out=out_rows[1][b][:, rows, :], in_=qk_out_tiles[n][:, 1, first : first + count, :])
 
         build_angles(0, TILES)
         build_tables(0)
@@ -310,18 +313,18 @@ def tile_spikinggroupedslidingattention_pa_t_kernel(
                 project_qk(u)
             if u >= V_LAG:
                 project_v(u - V_LAG)
+            if u < RUNS:
+                multiply_run(u)
             if u + AHEAD < RUNS:
                 quantise_run(u + AHEAD)
             if u < RUNS:
-                multiply_run(u)
                 n, run_in_block = divmod(u, RUNS_PER_BLOCK)
                 last_run_of_block = run_in_block == RUNS_PER_BLOCK - 1
-                if u == RUNS - 1:
-                    finish_qk(nc.vector, n, RUN * run_in_block, RUN)
-                elif n >= BLOCKS - TAIL_BLOCKS:
-                    finish_qk(nc.gpsimd, n, RUN * run_in_block, RUN)
+                add_run(nc.vector if u == RUNS - 1 else nc.gpsimd, u)
+                if n >= BLOCKS - TAIL_BLOCKS:
+                    store_qk(n, RUN * run_in_block, RUN)
                 elif last_run_of_block:
-                    finish_qk(nc.gpsimd, n, 0, TILES)
+                    store_qk(n, 0, TILES)
                 if last_run_of_block:
                     if n + X_BUFS < BLOCKS:
                         load_x(n + X_BUFS, 0, TILES)

import math
from contextlib import ExitStack

import concourse.mybir as mybir
from concourse.masks import make_identity

BF16 = mybir.dt.bfloat16
F32 = mybir.dt.float32
I32 = mybir.dt.int32
U32 = mybir.dt.uint32
U8 = mybir.dt.uint8
FP8X4 = mybir.dt.float8_e4m3fn_x4
ALU = mybir.AluOpType
ACT = mybir.ActivationFunctionType

B, S, D, DH = 4, 2048, 1024, 128
P = 128
PACK = 4
K_PASS = P * PACK
PASSES = D // K_PASS
ROWS_PER_PARTITION = S // P
TILES = 4
BLOCKS_PER_BATCH = ROWS_PER_PARTITION // TILES
BLOCKS = B * BLOCKS_PER_BATCH
RUN = 2
RUNS_PER_BLOCK = TILES // RUN
RUNS = BLOCKS * RUNS_PER_BLOCK
AHEAD = 2
X_BUFS = 8
HEAD_BLOCKS = 2
TAIL_BLOCKS = 2
SORTED = 1
FIRST_SORTED_RUN = 4
V_LAG = 4
HALF = DH // 2
FREQS = DH // 2
THETA = 10000.0
ROUND_MAGIC = 12582912.0

FLOPS = 2 * B * S * D * 3 * DH


def tile_spikinggroupedslidingattention_pa_t_kernel(
    tc, x, Wq_words, Wq_scales, Wk_words, Wk_scales, Wv_words, Wv_scales, out_0, out_1, out_2
):
    nc = tc.nc
    weights = ((Wq_words, Wq_scales), (Wk_words, Wk_scales), (Wv_words, Wv_scales))

    x_rows = [x[b].rearrange("(j a) k -> j a k", a=ROWS_PER_PARTITION) for b in range(B)]
    out_rows = [
        [o[b, 0].rearrange("(j a) i -> j a i", a=ROWS_PER_PARTITION) for b in range(B)]
        for o in (out_0, out_1, out_2)
    ]

    with ExitStack() as stack:
        const = stack.enter_context(tc.tile_pool(name="const", bufs=1))
        x_pool = stack.enter_context(tc.tile_pool(name="x_pool", bufs=X_BUFS))
        sorted_pool = stack.enter_context(tc.tile_pool(name="sorted_pool", bufs=3))
        grouped_pool = stack.enter_context(tc.tile_pool(name="grouped_pool", bufs=AHEAD + 1))
        quant = stack.enter_context(tc.tile_pool(name="quant", bufs=AHEAD + V_LAG + 2))
        rope = stack.enter_context(tc.tile_pool(name="rope", bufs=2))
        results = stack.enter_context(tc.tile_pool(name="results", bufs=3))
        last_v = stack.enter_context(tc.tile_pool(name="last_v", bufs=V_LAG))
        xt_banks = stack.enter_context(tc.psum_pool(name="xt_banks", bufs=AHEAD * RUN))
        qk_banks = stack.enter_context(tc.psum_pool(name="qk_banks", bufs=3))
        v_banks = stack.enter_context(tc.psum_pool(name="v_banks", bufs=1))
        stack.enter_context(tc.manual_schedule())

        x_tiles = {}

        def load_x(n, first, count):
            b, r = divmod(n, BLOCKS_PER_BATCH)
            if first == 0:
                x_tiles[n] = x_pool.tile([P, TILES, D], BF16, name="x_sb")
            nc.sync.dma_start(
                out=x_tiles[n][:, first : first + count, :],
                in_=x_rows[b][:, TILES * r + first : TILES * r + first + count, :],
            )

        position_int = const.tile([P, ROWS_PER_PARTITION], I32)
        nc.gpsimd.iota(position_int[:], pattern=[[1, ROWS_PER_PARTITION]], base=0, channel_multiplier=ROWS_PER_PARTITION)
        identity = const.tile([P, P], F32)
        make_identity(nc, identity[:])

        w_words = const.tile([P, PASSES, 3 * DH], U32, align_bytes=64)
        for w, (words, scales) in enumerate(weights):
            nc.gpsimd.dma_start(
                out=w_words[:, :, DH * w : DH * (w + 1)].bitcast(F32),
                in_=words.rearrange("g p n t -> p g (n t)").bitcast(F32),
            )

        w_scales = const.tile([P, PASSES, 3 * DH], U8, align_bytes=64)
        nc.vector.memset(w_scales[:].rearrange("p g n -> p (g n)").bitcast(I32), 0)

        load_x(0, 0, 1)
        load_x(0, 1, 1)
        load_x(0, RUN, RUN)
        load_x(1, 0, RUN)
        for w, (words, scales) in enumerate(weights):
            for quadrant in range(4):
                nc.sync.dma_start(
                    out=w_scales[32 * quadrant : 32 * quadrant + 4, :, DH * w : DH * (w + 1)].bitcast(I32),
                    in_=scales[:, 4 * quadrant : 4 * quadrant + 4, :].rearrange("g r n -> r g n").bitcast(I32),
                )
        load_x(1, RUN, RUN)
        for n in range(HEAD_BLOCKS, X_BUFS):
            load_x(n, 0, TILES)

        turns_per_step = const.tile([P, FREQS], F32)
        nc.vector.memset(turns_per_step[:], 1.0)
        nc.vector.tensor_scalar_mul(out=turns_per_step[:], in0=turns_per_step[:], scalar1=1.0 / (2.0 * math.pi))
        for bit in range(6):
            with_bit = turns_per_step[:].rearrange("p (h b l) -> p h b l", b=2, l=2**bit)[:, :, 1, :]
            nc.vector.tensor_scalar_mul(out=with_bit, in0=with_bit, scalar1=THETA ** (-(2.0**bit) / FREQS))
        quarter_turn = const.tile([P, 1], F32)
        nc.vector.memset(quarter_turn[:], 1.0)
        nc.vector.tensor_scalar_mul(out=quarter_turn[:], in0=quarter_turn[:], scalar1=math.pi / 2.0)
        position = const.tile([P, ROWS_PER_PARTITION], F32)
        nc.vector.tensor_copy(out=position[:], in_=position_int[:])

        cos_table = const.tile([P, ROWS_PER_PARTITION, DH], F32)
        sin_table = const.tile([P, ROWS_PER_PARTITION, DH], F32)

        turns = const.tile([P, ROWS_PER_PARTITION, FREQS], F32)
        whole = const.tile([P, ROWS_PER_PARTITION, FREQS], F32)
        part = const.tile([P, ROWS_PER_PARTITION, FREQS], F32)
        minus_abs = const.tile([P, ROWS_PER_PARTITION, FREQS], F32)

        def build_angles(first, count):
            tiles = slice(first, first + count)
            shape = [P, count, FREQS]
            nc.vector.tensor_tensor(
                out=turns[:, tiles, :],
                in0=position[:, tiles].unsqueeze(2).to_broadcast(shape),
                in1=turns_per_step[:].unsqueeze(1).to_broadcast(shape),
                op=ALU.mult,
            )
            nc.vector.tensor_scalar(
                out=whole[:, tiles, :],
                in0=turns[:, tiles, :],
                scalar1=ROUND_MAGIC,
                scalar2=ROUND_MAGIC,
                op0=ALU.add,
                op1=ALU.subtract,
            )
            nc.vector.tensor_tensor(out=part[:, tiles, :], in0=turns[:, tiles, :], in1=whole[:, tiles, :], op=ALU.subtract)
            nc.vector.scalar_tensor_tensor(
                out=minus_abs[:, tiles, :],
                in0=part[:, tiles, :],
                scalar=-1.0,
                in1=part[:, tiles, :],
                op0=ALU.mult,
                op1=ALU.min,
            )

        def build_tables(r):
            tiles = slice(TILES * r, TILES * (r + 1))
            nc.scalar.activation(
                out=cos_table[:, tiles, :].rearrange("p a (m e) -> p a m e", e=2),
                in_=minus_abs[:, tiles, :].unsqueeze(3).to_broadcast([P, TILES, FREQS, 2]),
                func=ACT.Sin,
                scale=2.0 * math.pi,
                bias=quarter_turn[:, 0:1],
            )
            half_shape = [P, TILES, FREQS // 2, 2]
            nc.scalar.activation(
                out=sin_table[:, tiles, 0:HALF].rearrange("p a (m e) -> p a m e", e=2),
                in_=part[:, tiles, FREQS // 2 : FREQS].unsqueeze(3).to_broadcast(half_shape),
                func=ACT.Sin,
                scale=2.0 * math.pi,
            )
            nc.scalar.activation(
                out=sin_table[:, tiles, HALF:DH].rearrange("p a (m e) -> p a m e", e=2),
                in_=part[:, tiles, 0 : FREQS // 2].unsqueeze(3).to_broadcast(half_shape),
                func=ACT.Sin,
                scale=-2.0 * math.pi,
            )

        grouped_tiles = {}
        x_codes = {}
        x_scales = {}
        qk_tiles = {}
        v_tiles = {}
        by_cos_tiles = {}
        by_sin_tiles = {}

        sorted_tiles = {}

        def sort_run(u):
            n, first = divmod(u * RUN, TILES)
            for a in range(SORTED):
                in_order = sorted_pool.tile([P, D // 2], F32, name="in_order")
                nc.scalar.copy(
                    out=in_order[:].rearrange("p (g o j) -> p g o j", g=PASSES, o=2),
                    in_=x_tiles[n][:, first + a, :].bitcast(F32).rearrange("p (g j o) -> p g o j", g=PASSES, o=2),
                )
                sorted_tiles[(u, a)] = in_order

        def transpose_run(u):
            n, first = divmod(u * RUN, TILES)
            grouped = grouped_pool.tile([P, RUN, D], BF16, name="grouped", align_bytes=64)
            for a in range(RUN):
                pairs = x_tiles[n][:, first + a, :].bitcast(F32)
                xt = xt_banks.tile([P, 2 * PASSES, P], F32, name="xt")
                for g in range(PASSES):
                    for odd in range(2):
                        if (u, a) in sorted_tiles:
                            words = sorted_tiles[(u, a)][:, P * (2 * g + odd) : P * (2 * g + odd + 1)]
                        else:
                            words = pairs[:, 256 * g + odd : 256 * (g + 1) : 2]
                        nc.tensor.transpose(xt[:, 2 * g + odd, :], words, identity[:])
                nc.scalar.copy(
                    out=grouped[:, a, :].bitcast(F32).rearrange("p (g j o) -> p g j o", g=PASSES, o=2),
                    in_=xt[:].rearrange("p (g o) j -> p g j o", o=2),
                )
            grouped_tiles[u] = grouped

        def quantise_run(u):
            codes = quant.tile([P, RUN * PASSES * P], U32, name="codes", align_bytes=64)
            scales = quant.tile([P, RUN * PASSES * P], U8, name="scales", align_bytes=64)
            nc.vector.quantize_mx(
                out=codes[:].bitcast(FP8X4), scales=scales[:], in_=grouped_tiles[u][:].rearrange("p a c -> p (a c)")
            )
            x_codes[u] = codes
            x_scales[u] = scales

        def project(u, a, out, columns):
            for g in range(PASSES):
                rows = slice((a * PASSES + g) * P, (a * PASSES + g + 1) * P)
                nc.tensor.matmul_mx(
                    out=out,
                    lhsT=x_codes[u][:, rows].bitcast(FP8X4),
                    lhsT_scale=x_scales[u][:, rows],
                    rhs=w_words[:, g, columns].bitcast(FP8X4),
                    rhs_scale=w_scales[:, g, columns],
                    start=(g == 0),
                    stop=(g == PASSES - 1),
                )

        def project_qk(u):
            qk_bank = qk_banks.tile([P, RUN, 2 * DH], F32, name="qk_bank")
            for a in range(RUN):
                project(u, a, qk_bank[:, a, :], slice(0, 2 * DH))
            qk_tiles[u] = qk_bank

        def project_v(u):
            n, first = divmod(u * RUN, TILES)
            b, r = divmod(n, BLOCKS_PER_BATCH)
            if u >= RUNS - V_LAG:
                v_bank = xt_banks.tile([P, RUN, DH], F32, name="xt")
                for a in range(RUN):
                    project(u, a, v_bank[:, a, :], slice(2 * DH, 3 * DH))
                v_last = last_v.tile([P, RUN, DH], F32, name="v_last")
                nc.scalar.copy(out=v_last[:], in_=v_bank[:])
                nc.sync.dma_start(out=out_rows[2][b][:, TILES * r + first : TILES * r + first + RUN, :], in_=v_last[:])
                return
            if first == 0:
                v_tiles[n] = v_banks.tile([P, TILES, DH], F32, name="v_bank")
            for a in range(RUN):
                project(u, a, v_tiles[n][:, first + a, :], slice(2 * DH, 3 * DH))
            if first + RUN == TILES:
                v_out = results.tile([P, TILES, DH], F32, name="v_out")
                nc.scalar.copy(out=v_out[:], in_=v_tiles[n][:])
                nc.sync.dma_start(out=out_rows[2][b][:, TILES * r : TILES * (r + 1), :], in_=v_out[:])

        def multiply_run(u):
            n, first = divmod(u * RUN, TILES)
            if first == 0:
                by_cos_tiles[n] = rope.tile([P, TILES, 2, DH], F32, name="by_cos")
                by_sin_tiles[n] = rope.tile([P, TILES, 2, DH], F32, name="by_sin")
            table_first = TILES * (n % BLOCKS_PER_BATCH) + first
            for product, table in ((by_cos_tiles[n], cos_table), (by_sin_tiles[n], sin_table)):
                nc.vector.tensor_tensor(
                    out=product[:, first : first + RUN, :, :],
                    in0=qk_tiles[u][:].rearrange("p a (s i) -> p a s i", s=2),
                    in1=table[:, table_first : table_first + RUN, :].unsqueeze(2).to_broadcast([P, RUN, 2, DH]),
                    op=ALU.mult,
                )

        qk_out_tiles = {}

        def add_run(engine, u):
            n, first = divmod(u * RUN, TILES)
            if first == 0:
                qk_out_tiles[n] = results.tile([P, 2, TILES, DH], F32, name="qk_out")
            tiles = slice(first, first + RUN)
            engine.tensor_tensor(
                out=qk_out_tiles[n][:, :, tiles, :].rearrange("p s a (h i) -> p a s h i", h=2),
                in0=by_cos_tiles[n][:, tiles, :, :].rearrange("p a s (h i) -> p a s h i", h=2),
                in1=by_sin_tiles[n][:, tiles, :, :].rearrange("p a s (h i) -> p a s h i", h=2)[:, :, :, ::-1, :],
                op=ALU.add,
            )

        def store_qk(n, first, count):
            b, r = divmod(n, BLOCKS_PER_BATCH)
            rows = slice(TILES * r + first, TILES * r + first + count)
            nc.sync.dma_start(out=out_rows[0][b][:, rows, :], in_=qk_out_tiles[n][:, 0, first : first + count, :])
            nc.sync.dma_start(out=out_rows[1][b][:, rows, :], in_=qk_out_tiles[n][:, 1, first : first + count, :])

        build_angles(0, TILES)
        build_tables(0)
        build_angles(TILES, ROWS_PER_PARTITION - TILES)
        for u in range(AHEAD):
            transpose_run(u)
        for u in range(AHEAD):
            quantise_run(u)
        for u in range(RUNS + V_LAG):
            if FIRST_SORTED_RUN <= u + AHEAD + 1 < RUNS and (u + AHEAD + 1) % RUNS_PER_BLOCK == 0:
                sort_run(u + AHEAD + 1)
            if u + AHEAD < RUNS:
                transpose_run(u + AHEAD)
            if u < RUNS:
                project_qk(u)
            if u >= V_LAG:
                project_v(u - V_LAG)
            if u < RUNS:
                multiply_run(u)
            if u + AHEAD < RUNS:
                quantise_run(u + AHEAD)
            if u < RUNS:
                n, run_in_block = divmod(u, RUNS_PER_BLOCK)
                last_run_of_block = run_in_block == RUNS_PER_BLOCK - 1
                add_run(nc.vector if u == RUNS - 1 else nc.gpsimd, u)
                if n >= BLOCKS - TAIL_BLOCKS:
                    store_qk(n, RUN * run_in_block, RUN)
                elif last_run_of_block:
                    store_qk(n, 0, TILES)
                if last_run_of_block:
                    if n + X_BUFS < BLOCKS:
                        load_x(n + X_BUFS, 0, TILES)
                    if n + 1 < BLOCKS_PER_BATCH:
                        build_tables(n + 1)
